import numpy as np
import ml_dtypes


def mxq(x, axis, fmt="e4m3"):
    dtype, down = {"e4m3": (ml_dtypes.float8_e4m3fn, 7), "e5m2": (ml_dtypes.float8_e5m2, 14)}[fmt]
    v = np.moveaxis(np.asarray(x, np.float32).astype(ml_dtypes.bfloat16).astype(np.float64), axis, -1)
    blocks = v.reshape(v.shape[:-1] + (-1, 32))
    amax = np.abs(blocks).max(-1, keepdims=True)
    byte = np.maximum(np.where(amax > 0, np.frexp(amax)[1] - 1 + 127, 0) - down, 1)
    scale = np.exp2(byte - 127.0)
    codes = (blocks / scale).astype(np.float32).astype(dtype).astype(np.float64)
    return np.moveaxis((codes * scale).reshape(v.shape), -1, axis)


WIDE = False


def mx_kscale(k):
    if not WIDE:
        return np.ones(k)
    levels = np.array([10, -10, 5, -5, 0])
    a = np.random.permutation(np.resize(levels, k // 512 * 4)).reshape(k // 512, 4)
    idx = np.arange(k)
    return np.exp2(a[idx // 512, idx % 128 // 32])


BF16 = ml_dtypes.bfloat16


def bf(x):
    return np.asarray(x, np.float32).astype(BF16)


def f64(x):
    return np.asarray(x).astype(np.float64)


E2M1 = np.array([0.0, 0.5, 1.0, 1.5, 2.0, 3.0, 4.0, 6.0, -0.0, -0.5, -1.0, -1.5, -2.0, -3.0, -4.0, -6.0])


def pack_weight(w, fmt):
    k, n = w.shape
    w = f64(bf(w)).reshape(k // 32, 32, n)
    amax = np.abs(w).max(1)
    if fmt == "e4m3":
        byte = np.frexp(amax)[1] - 1 + 127 - 7
    else:
        mant, ex = np.frexp(amax / 6.0)
        byte = np.where(mant > 0.5, ex, ex - 1) + 127
    byte = np.clip(np.where(amax > 0, byte, 1), 1, 254)
    scaled = (w * np.exp2(127.0 - byte)[:, None, :]).reshape(k, n).astype(np.float32)
    by_word = np.ascontiguousarray(scaled.reshape(k // 512, 128, 4, n).transpose(0, 1, 3, 2))
    if fmt == "e4m3":
        words = by_word.astype(ml_dtypes.float8_e4m3fn).view(np.uint8)
    else:
        c = by_word.astype(ml_dtypes.float4_e2m1fn).view(np.uint8) & 0xF
        words = c[..., 0::2] | (c[..., 1::2] << 4)
    return np.ascontiguousarray(words), np.ascontiguousarray(byte.astype(np.uint8).reshape(k // 512, 16, n))


def unpack_weight(words, scales, fmt):
    g, p, n, _ = words.shape
    if fmt == "e4m3":
        vals = np.ascontiguousarray(words).view(ml_dtypes.float8_e4m3fn).astype(np.float64)
    else:
        nib = np.empty((g, p, n, 4), np.uint8)
        nib[..., 0::2] = words & 0xF
        nib[..., 1::2] = words >> 4
        vals = E2M1[nib]
    vals = vals * np.repeat(np.exp2(scales.astype(np.float64) - 127.0), 8, axis=1)[..., None]
    return vals.transpose(0, 1, 3, 2).reshape(g * 512, n)


B, N, VD, QD, D, H, NG, P = 128, 36, 2048, 1024, 512, 2, 20, 64
DH = D // H


def setup_inputs():
    s = mx_kscale(D)
    out_t = bf(np.random.standard_normal((B, N, H, D)) * 0.7 * s)
    stack = np.random.standard_normal((H, D, DH)) / np.sqrt(D) / s[None, :, None]
    words, scales = pack_weight(stack.reshape(-1, DH), "e4m3")
    return {"out_t": out_t,
            "out_w_words": words,
            "out_w_scales": scales,
            "out_b": bf(np.random.standard_normal(D) * 0.3),
            "self_feat": bf(np.random.standard_normal((B, N, D)) * 0.9),
            "vis": bf(np.maximum(np.random.standard_normal((B, N, D)), 0.0))}


def reference(out_t, out_w_words, out_w_scales, out_b, self_feat, vis):
    t = mxq(f64(out_t), 3, "e4m3").reshape(B * N, H, D).swapaxes(0, 1)
    nb = t @ unpack_weight(out_w_words, out_w_scales, "e4m3").reshape(H, D, DH)
    neighbor = nb.swapaxes(0, 1).reshape(B, N, D) + f64(out_b)
    imp_rel = np.maximum(f64(self_feat) + neighbor, 0.0)
    return f64(vis) + imp_rel

@@ -1,0 +1,190 @@
+from contextlib import ExitStack
+
+import concourse.mybir as mybir
+from concourse.masks import make_identity
+
+BF16 = mybir.dt.bfloat16
+F32 = mybir.dt.float32
+I32 = mybir.dt.int32
+U32 = mybir.dt.uint32
+U8 = mybir.dt.uint8
+FP8X4 = mybir.dt.float8_e4m3fn_x4
+ADD = mybir.AluOpType.add
+MAX = mybir.AluOpType.max
+
+P = 128
+OBJECTS = 36
+HEADS = 2
+D = 512
+DH = 256
+WIDTH = HEADS * DH
+HALVES = 2
+GROUP = 4
+PAIR = 2
+GROUPS = OBJECTS // GROUP
+PAIRS = OBJECTS // PAIR
+PAIRS_PER_GROUP = GROUP // PAIR
+AHEAD = 3
+
+FLOPS = 2 * P * OBJECTS * HEADS * D * DH
+
+
+def tile_implicitrelationencoder_pb_t_e_kernel(
+    tc, out_t, out_w_words, out_w_scales, out_b, self_feat, vis, out
+):
+    nc = tc.nc
+    with ExitStack() as ctx:
+        const = ctx.enter_context(tc.tile_pool(name="const", bufs=1))
+        x_pool = ctx.enter_context(tc.tile_pool(name="x", bufs=AHEAD + 1))
+        self_pool = ctx.enter_context(tc.tile_pool(name="self", bufs=AHEAD + 2))
+        vis_pool = ctx.enter_context(tc.tile_pool(name="vis", bufs=AHEAD + 2))
+        acc_pool = ctx.enter_context(tc.tile_pool(name="acc", bufs=3))
+        mx_pool = ctx.enter_context(tc.tile_pool(name="mx", bufs=3))
+        bias_psum = ctx.enter_context(tc.psum_pool(name="bias_psum", bufs=1))
+        xt_psum = ctx.enter_context(tc.psum_pool(name="xt_psum", bufs=3))
+        prod_psum = ctx.enter_context(tc.psum_pool(name="prod_psum", bufs=4))
+        ctx.enter_context(tc.manual_schedule())
+
+        x_of, self_of, vis_of, acc_of = {}, {}, {}, {}
+        xt_of, codes_of, scales_of, grouped_of, prod_of = {}, {}, {}, {}, {}
+
+        def load_group(g):
+            objs = slice(g * GROUP, (g + 1) * GROUP)
+            x_sb = x_pool.tile([P, GROUP, HEADS * D], BF16)
+            nc.sync.dma_start(out=x_sb[:], in_=out_t[:, objs].rearrange("b n h d -> b n (h d)"))
+            x_of[g] = x_sb
+            if g == 0:
+                load_weight()
+            self_sb = self_pool.tile([P, GROUP, WIDTH], BF16)
+            nc.sync.dma_start(out=self_sb[:], in_=self_feat[:, objs, :])
+            self_of[g] = self_sb
+            vis_sb = vis_pool.tile([P, GROUP, WIDTH], BF16)
+            nc.sync.dma_start(out=vis_sb[:], in_=vis[:, objs, :])
+            vis_of[g] = vis_sb
+
+        w_codes = const.tile([P, HEADS, DH], U32, align_bytes=64)
+        w_scales = const.tile([P, HEADS, DH], U8, align_bytes=64)
+        bias_row = const.tile([P, WIDTH], BF16)
+        ones = const.tile([P, P], BF16)
+        ident = const.tile([P, P], F32)
+
+        def load_weight():
+            for h in range(HEADS):
+                nc.sync.dma_start(
+                    out=w_codes[:, h, :].bitcast(I32),
+                    in_=out_w_words[h].rearrange("p n t -> p (n t)").bitcast(I32),
+                )
+            for quadrant in range(4):
+                nc.sync.dma_start(
+                    out=w_scales[32 * quadrant : 32 * quadrant + 4].bitcast(I32),
+                    in_=out_w_scales[:, 4 * quadrant : 4 * quadrant + 4, :]
+                    .rearrange("h q n -> q h n")
+                    .bitcast(I32),
+                )
+            nc.sync.dma_start(out=bias_row[0:1, :], in_=out_b.unsqueeze(0))
+
+        def transpose_pair(n):
+            g, half = divmod(n, PAIRS_PER_GROUP)
+            x_words = x_of[g][:].bitcast(F32)
+            for j in range(PAIR):
+                xt = xt_psum.tile([P, HEADS, HALVES, P], F32)
+                for h in range(HEADS):
+                    for u in range(HALVES):
+                        first = h * (D // 2) + u
+                        nc.tensor.transpose(
+                            xt[:, h, u, :],
+                            x_words[:, half * PAIR + j, first : (h + 1) * (D // 2) : HALVES],
+                            ident[:],
+                        )
+                xt_of[n, j] = xt
+
+        def regroup_pair(n):
+            grouped = mx_pool.tile([P, PAIR, HEADS, P, 2 * HALVES], BF16, align_bytes=64)
+            for j in range(PAIR):
+                nc.scalar.copy(
+                    out=grouped[:].bitcast(F32)[:, j],
+                    in_=xt_of[n, j][:].rearrange("k h u r -> k h r u"),
+                )
+            grouped_of[n] = grouped
+
+        def quantise_pair(n):
+            codes = mx_pool.tile([P, PAIR, HEADS, P], U32, align_bytes=64)
+            scales = mx_pool.tile([P, PAIR, HEADS, P], U8, align_bytes=64)
+            nc.vector.quantize_mx(
+                out=codes[:].rearrange("k j h r -> k (j h r)").bitcast(FP8X4),
+                scales=scales[:].rearrange("k j h r -> k (j h r)"),
+                in_=grouped_of[n][:].rearrange("k j h r t -> k (j h r t)"),
+            )
+            codes_of[n], scales_of[n] = codes, scales
+
+        def multiply_pair(n):
+            for j in range(PAIR):
+                prod = prod_psum.tile([P, HEADS, DH], F32)
+                for h in range(HEADS):
+                    nc.tensor.matmul_mx(
+                        out=prod[:, h, :],
+                        lhsT=codes_of[n][:, j, h, :].bitcast(FP8X4),
+                        lhsT_scale=scales_of[n][:, j, h, :],
+                        rhs=w_codes[:, h, :].bitcast(FP8X4),
+                        rhs_scale=w_scales[:, h, :],
+                        start=True,
+                        stop=True,
+                    )
+                prod_of[n, j] = prod
+
+        def add_bias_pair(n):
+            g, half = divmod(n, PAIRS_PER_GROUP)
+            if half == 0:
+                acc = acc_pool.tile([P, GROUP, WIDTH], F32)
+                acc_of[g] = acc
+            objs = slice(half * PAIR, (half + 1) * PAIR)
+            nc.vector.tensor_tensor(
+                out=acc_of[g][:, objs, :],
+                in0=self_of[g][:, objs, :],
+                in1=bias_all[:].unsqueeze(1).to_broadcast([P, PAIR, WIDTH]),
+                op=ADD,
+            )
+
+        def finish_pair(n):
+            g, half = divmod(n, PAIRS_PER_GROUP)
+            for j in range(PAIR):
+                acc_row = acc_of[g][:, half * PAIR + j, :]
+                nc.vector.tensor_tensor(
+                    out=acc_row,
+                    in0=prod_of[n, j][:].rearrange("b h c -> b (h c)"),
+                    in1=acc_row,
+                    op=ADD,
+                )
+            for j in range(PAIR):
+                obj = half * PAIR + j
+                acc_row = acc_of[g][:, obj, :]
+                nc.vector.scalar_tensor_tensor(
+                    out=acc_row, in0=acc_row, scalar=0.0, in1=vis_of[g][:, obj, :], op0=MAX, op1=ADD
+                )
+            if half == PAIRS_PER_GROUP - 1:
+                nc.sync.dma_start(out=out[:, g * GROUP : (g + 1) * GROUP, :], in_=acc_of[g][:])
+
+        nc.vector.memset(w_scales[:].bitcast(I32), 0)
+        nc.vector.memset(bias_row[:], 0.0)
+        nc.vector.memset(ones[:], 1.0)
+        make_identity(nc, ident[:])
+
+        for g in range(AHEAD):
+            load_group(g)
+
+        bias_all = bias_psum.tile([P, WIDTH], F32)
+        for n in range(PAIRS + 2):
+            if n < PAIRS:
+                g, half = divmod(n, PAIRS_PER_GROUP)
+                if half == 0 and g + AHEAD < GROUPS:
+                    load_group(g + AHEAD)
+                transpose_pair(n)
+                regroup_pair(n)
+                if n == 1:
+                    nc.tensor.matmul(out=bias_all[:], lhsT=ones[:], rhs=bias_row[:], start=True, stop=True)
+            if 1 <= n <= PAIRS:
+                quantise_pair(n - 1)
+                multiply_pair(n - 1)
+                add_bias_pair(n - 1)
+            if n >= 2:
+                finish_pair(n - 2)

@@ -10,7 +10,7 @@ U32 = mybir.dt.uint32
 U8 = mybir.dt.uint8
 FP8X4 = mybir.dt.float8_e4m3fn_x4
 ADD = mybir.AluOpType.add
-MAX = mybir.AluOpType.max
+RELU = mybir.ActivationFunctionType.Relu
 
 P = 128
 OBJECTS = 36
@@ -155,12 +155,10 @@ def tile_implicitrelationencoder_pb_t_e_kernel(
                     in1=acc_row,
                     op=ADD,
                 )
-            for j in range(PAIR):
-                obj = half * PAIR + j
-                acc_row = acc_of[g][:, obj, :]
-                nc.vector.scalar_tensor_tensor(
-                    out=acc_row, in0=acc_row, scalar=0.0, in1=vis_of[g][:, obj, :], op0=MAX, op1=ADD
-                )
+            objs = slice(half * PAIR, (half + 1) * PAIR)
+            acc_pair = acc_of[g][:, objs, :]
+            nc.scalar.activation(out=acc_pair, in_=acc_pair, func=RELU)
+            nc.gpsimd.tensor_tensor(out=acc_pair, in0=acc_pair, in1=vis_of[g][:, objs, :], op=ADD)
             if half == PAIRS_PER_GROUP - 1:
                 nc.sync.dma_start(out=out[:, g * GROUP : (g + 1) * GROUP, :], in_=acc_of[g][:])
 

@@ -24,7 +24,7 @@ PAIR = 2
 GROUPS = OBJECTS // GROUP
 PAIRS = OBJECTS // PAIR
 PAIRS_PER_GROUP = GROUP // PAIR
-AHEAD = 3
+AHEAD = 4
 
 FLOPS = 2 * P * OBJECTS * HEADS * D * DH
 
@@ -38,7 +38,7 @@ def tile_implicitrelationencoder_pb_t_e_kernel(
         x_pool = ctx.enter_context(tc.tile_pool(name="x", bufs=AHEAD + 1))
         self_pool = ctx.enter_context(tc.tile_pool(name="self", bufs=AHEAD + 2))
         vis_pool = ctx.enter_context(tc.tile_pool(name="vis", bufs=AHEAD + 2))
-        acc_pool = ctx.enter_context(tc.tile_pool(name="acc", bufs=3))
+        acc_pool = ctx.enter_context(tc.tile_pool(name="acc", bufs=GROUPS))
         mx_pool = ctx.enter_context(tc.tile_pool(name="mx", bufs=3))
         bias_psum = ctx.enter_context(tc.psum_pool(name="bias_psum", bufs=1))
         xt_psum = ctx.enter_context(tc.psum_pool(name="xt_psum", bufs=3))
@@ -159,8 +159,6 @@ def tile_implicitrelationencoder_pb_t_e_kernel(
             acc_pair = acc_of[g][:, objs, :]
             nc.scalar.activation(out=acc_pair, in_=acc_pair, func=RELU)
             nc.gpsimd.tensor_tensor(out=acc_pair, in0=acc_pair, in1=vis_of[g][:, objs, :], op=ADD)
-            if half == PAIRS_PER_GROUP - 1:
-                nc.sync.dma_start(out=out[:, g * GROUP : (g + 1) * GROUP, :], in_=acc_of[g][:])
 
         nc.vector.memset(w_scales[:].bitcast(I32), 0)
         nc.vector.memset(bias_row[:], 0.0)
@@ -186,3 +184,6 @@ def tile_implicitrelationencoder_pb_t_e_kernel(
                 add_bias_pair(n - 1)
             if n >= 2:
                 finish_pair(n - 2)
+
+        for g in range(GROUPS):
+            nc.sync.dma_start(out=out[:, g * GROUP : (g + 1) * GROUP, :], in_=acc_of[g][:])

@@ -181,9 +181,10 @@ def tile_implicitrelationencoder_pb_t_e_kernel(
             if 1 <= n <= PAIRS:
                 quantise_pair(n - 1)
                 multiply_pair(n - 1)
-                add_bias_pair(n - 1)
             if n >= 2:
                 finish_pair(n - 2)
+            if 1 <= n <= PAIRS:
+                add_bias_pair(n - 1)
 
         for g in range(GROUPS):
             nc.sync.dma_start(out=out[:, g * GROUP : (g + 1) * GROUP, :], in_=acc_of[g][:])

@@ -10,6 +10,7 @@ U32 = mybir.dt.uint32
 U8 = mybir.dt.uint8
 FP8X4 = mybir.dt.float8_e4m3fn_x4
 ADD = mybir.AluOpType.add
+MAX = mybir.AluOpType.max
 RELU = mybir.ActivationFunctionType.Relu
 
 P = 128
@@ -18,13 +19,13 @@ HEADS = 2
 D = 512
 DH = 256
 WIDTH = HEADS * DH
+CODES = 4
 HALVES = 2
-GROUP = 4
+D_WORDS = D // 2
+QUADRANTS = 4
 PAIR = 2
-GROUPS = OBJECTS // GROUP
 PAIRS = OBJECTS // PAIR
-PAIRS_PER_GROUP = GROUP // PAIR
-AHEAD = 4
+AHEAD = 8
 
 FLOPS = 2 * P * OBJECTS * HEADS * D * DH
 
@@ -35,10 +36,10 @@ def tile_implicitrelationencoder_pb_t_e_kernel(
     nc = tc.nc
     with ExitStack() as ctx:
         const = ctx.enter_context(tc.tile_pool(name="const", bufs=1))
-        x_pool = ctx.enter_context(tc.tile_pool(name="x", bufs=AHEAD + 1))
+        x_pool = ctx.enter_context(tc.tile_pool(name="x", bufs=AHEAD + 3))
         self_pool = ctx.enter_context(tc.tile_pool(name="self", bufs=AHEAD + 2))
-        vis_pool = ctx.enter_context(tc.tile_pool(name="vis", bufs=AHEAD + 2))
-        acc_pool = ctx.enter_context(tc.tile_pool(name="acc", bufs=GROUPS))
+        vis_pool = ctx.enter_context(tc.tile_pool(name="vis", bufs=AHEAD + 3))
+        acc_pool = ctx.enter_context(tc.tile_pool(name="acc", bufs=PAIRS))
         mx_pool = ctx.enter_context(tc.tile_pool(name="mx", bufs=3))
         bias_psum = ctx.enter_context(tc.psum_pool(name="bias_psum", bufs=1))
         xt_psum = ctx.enter_context(tc.psum_pool(name="xt_psum", bufs=3))
@@ -46,64 +47,71 @@ def tile_implicitrelationencoder_pb_t_e_kernel(
         ctx.enter_context(tc.manual_schedule())
 
         x_of, self_of, vis_of, acc_of = {}, {}, {}, {}
-        xt_of, codes_of, scales_of, grouped_of, prod_of = {}, {}, {}, {}, {}
-
-        def load_group(g):
-            objs = slice(g * GROUP, (g + 1) * GROUP)
-            x_sb = x_pool.tile([P, GROUP, HEADS * D], BF16)
-            nc.sync.dma_start(out=x_sb[:], in_=out_t[:, objs].rearrange("b n h d -> b n (h d)"))
-            x_of[g] = x_sb
-            if g == 0:
-                load_weight()
-            self_sb = self_pool.tile([P, GROUP, WIDTH], BF16)
-            nc.sync.dma_start(out=self_sb[:], in_=self_feat[:, objs, :])
-            self_of[g] = self_sb
-            vis_sb = vis_pool.tile([P, GROUP, WIDTH], BF16)
-            nc.sync.dma_start(out=vis_sb[:], in_=vis[:, objs, :])
-            vis_of[g] = vis_sb
+        xt_of, grouped_of, codes_of, scales_of, prod_of = {}, {}, {}, {}, {}
 
         w_codes = const.tile([P, HEADS, DH], U32, align_bytes=64)
         w_scales = const.tile([P, HEADS, DH], U8, align_bytes=64)
         bias_row = const.tile([P, WIDTH], BF16)
         ones = const.tile([P, P], BF16)
         ident = const.tile([P, P], F32)
+        bias_all = bias_psum.tile([P, WIDTH], F32)
+
+        nc.vector.memset(w_scales[:].bitcast(I32), 0)
+        nc.vector.memset(bias_row[:], 0.0)
+        nc.vector.memset(ones[:], 1.0)
+        make_identity(nc, ident[:])
 
         def load_weight():
-            for h in range(HEADS):
-                nc.sync.dma_start(
-                    out=w_codes[:, h, :].bitcast(I32),
-                    in_=out_w_words[h].rearrange("p n t -> p (n t)").bitcast(I32),
-                )
-            for quadrant in range(4):
+            nc.sync.dma_start(
+                out=w_codes[:].bitcast(I32),
+                in_=out_w_words.rearrange("h p c t -> p h (c t)").bitcast(I32),
+            )
+            for quadrant in range(QUADRANTS):
                 nc.sync.dma_start(
                     out=w_scales[32 * quadrant : 32 * quadrant + 4].bitcast(I32),
                     in_=out_w_scales[:, 4 * quadrant : 4 * quadrant + 4, :]
-                    .rearrange("h q n -> q h n")
+                    .rearrange("h q c -> q h c")
                     .bitcast(I32),
                 )
-            nc.sync.dma_start(out=bias_row[0:1, :], in_=out_b.unsqueeze(0))
+
+        def spread_bias():
+            nc.tensor.matmul(out=bias_all[:], lhsT=ones[:], rhs=bias_row[:], start=True, stop=True)
+
+        def objects(n):
+            return slice(n * PAIR, (n + 1) * PAIR)
+
+        def load_x(n):
+            x_sb = x_pool.tile([P, PAIR, HEADS * D], BF16)
+            nc.sync.dma_start(out=x_sb[:], in_=out_t[:, objects(n)].rearrange("b n h k -> b n (h k)"))
+            x_of[n] = x_sb
+
+        def load_residuals(n):
+            self_sb = self_pool.tile([P, PAIR, WIDTH], BF16)
+            nc.sync.dma_start(out=self_sb[:], in_=self_feat[:, objects(n), :])
+            self_of[n] = self_sb
+            vis_sb = vis_pool.tile([P, PAIR, WIDTH], BF16)
+            nc.sync.dma_start(out=vis_sb[:], in_=vis[:, objects(n), :])
+            vis_of[n] = vis_sb
 
         def transpose_pair(n):
-            g, half = divmod(n, PAIRS_PER_GROUP)
-            x_words = x_of[g][:].bitcast(F32)
+            x_words = x_of[n][:].bitcast(F32)
             for j in range(PAIR):
                 xt = xt_psum.tile([P, HEADS, HALVES, P], F32)
                 for h in range(HEADS):
                     for u in range(HALVES):
-                        first = h * (D // 2) + u
                         nc.tensor.transpose(
                             xt[:, h, u, :],
-                            x_words[:, half * PAIR + j, first : (h + 1) * (D // 2) : HALVES],
+                            x_words[:, j, h * D_WORDS + u : (h + 1) * D_WORDS : HALVES],
                             ident[:],
                         )
                 xt_of[n, j] = xt
 
         def regroup_pair(n):
-            grouped = mx_pool.tile([P, PAIR, HEADS, P, 2 * HALVES], BF16, align_bytes=64)
+            grouped = mx_pool.tile([P, PAIR, HEADS, P, CODES], BF16, align_bytes=64)
             for j in range(PAIR):
                 nc.scalar.copy(
                     out=grouped[:].bitcast(F32)[:, j],
-                    in_=xt_of[n, j][:].rearrange("k h u r -> k h r u"),
+                    in_=xt_of[n, j][:].rearrange("p h u b -> p h b u"),
                 )
             grouped_of[n] = grouped
 
@@ -111,9 +119,9 @@ def tile_implicitrelationencoder_pb_t_e_kernel(
             codes = mx_pool.tile([P, PAIR, HEADS, P], U32, align_bytes=64)
             scales = mx_pool.tile([P, PAIR, HEADS, P], U8, align_bytes=64)
             nc.vector.quantize_mx(
-                out=codes[:].rearrange("k j h r -> k (j h r)").bitcast(FP8X4),
-                scales=scales[:].rearrange("k j h r -> k (j h r)"),
-                in_=grouped_of[n][:].rearrange("k j h r t -> k (j h r t)"),
+                out=codes[:].rearrange("p j h b -> p (j h b)").bitcast(FP8X4),
+                scales=scales[:].rearrange("p j h b -> p (j h b)"),
+                in_=grouped_of[n][:].rearrange("p j h b t -> p (j h b t)"),
             )
             codes_of[n], scales_of[n] = codes, scales
 
@@ -133,58 +141,62 @@ def tile_implicitrelationencoder_pb_t_e_kernel(
                 prod_of[n, j] = prod
 
         def add_bias_pair(n):
-            g, half = divmod(n, PAIRS_PER_GROUP)
-            if half == 0:
-                acc = acc_pool.tile([P, GROUP, WIDTH], F32)
-                acc_of[g] = acc
-            objs = slice(half * PAIR, (half + 1) * PAIR)
+            acc = acc_pool.tile([P, PAIR, WIDTH], F32)
             nc.vector.tensor_tensor(
-                out=acc_of[g][:, objs, :],
-                in0=self_of[g][:, objs, :],
+                out=acc[:],
+                in0=self_of[n][:],
                 in1=bias_all[:].unsqueeze(1).to_broadcast([P, PAIR, WIDTH]),
                 op=ADD,
             )
+            acc_of[n] = acc
 
-        def finish_pair(n):
-            g, half = divmod(n, PAIRS_PER_GROUP)
+        def add_product_pair(n):
             for j in range(PAIR):
-                acc_row = acc_of[g][:, half * PAIR + j, :]
                 nc.vector.tensor_tensor(
-                    out=acc_row,
+                    out=acc_of[n][:, j, :],
                     in0=prod_of[n, j][:].rearrange("b h c -> b (h c)"),
-                    in1=acc_row,
+                    in1=acc_of[n][:, j, :],
                     op=ADD,
                 )
-            objs = slice(half * PAIR, (half + 1) * PAIR)
-            acc_pair = acc_of[g][:, objs, :]
-            nc.scalar.activation(out=acc_pair, in_=acc_pair, func=RELU)
-            nc.gpsimd.tensor_tensor(out=acc_pair, in0=acc_pair, in1=vis_of[g][:, objs, :], op=ADD)
 
-        nc.vector.memset(w_scales[:].bitcast(I32), 0)
-        nc.vector.memset(bias_row[:], 0.0)
-        nc.vector.memset(ones[:], 1.0)
-        make_identity(nc, ident[:])
+        def relu_add_vis_pair(n):
+            nc.scalar.activation(out=acc_of[n][:], in_=acc_of[n][:], func=RELU)
+            nc.gpsimd.tensor_tensor(out=acc_of[n][:], in0=acc_of[n][:], in1=vis_of[n][:], op=ADD)
 
-        for g in range(AHEAD):
-            load_group(g)
+        def relu_add_vis_last_pair(n):
+            nc.vector.scalar_tensor_tensor(
+                out=acc_of[n][:], in0=acc_of[n][:], scalar=0.0, in1=vis_of[n][:], op0=MAX, op1=ADD
+            )
 
-        bias_all = bias_psum.tile([P, WIDTH], F32)
-        for n in range(PAIRS + 2):
-            if n < PAIRS:
-                g, half = divmod(n, PAIRS_PER_GROUP)
-                if half == 0 and g + AHEAD < GROUPS:
-                    load_group(g + AHEAD)
-                transpose_pair(n)
-                regroup_pair(n)
-                if n == 1:
-                    nc.tensor.matmul(out=bias_all[:], lhsT=ones[:], rhs=bias_row[:], start=True, stop=True)
-            if 1 <= n <= PAIRS:
-                quantise_pair(n - 1)
-                multiply_pair(n - 1)
-            if n >= 2:
-                finish_pair(n - 2)
-            if 1 <= n <= PAIRS:
-                add_bias_pair(n - 1)
+        load_x(0)
+        load_weight()
+        load_x(1)
+        nc.sync.dma_start(out=bias_row[0:1, :], in_=out_b.unsqueeze(0))
+        for n in range(AHEAD):
+            load_residuals(n)
+            load_x(n + 2)
 
-        for g in range(GROUPS):
-            nc.sync.dma_start(out=out[:, g * GROUP : (g + 1) * GROUP, :], in_=acc_of[g][:])
+        for step in range(PAIRS + 2):
+            if step + AHEAD < PAIRS:
+                load_residuals(step + AHEAD)
+            if step + AHEAD + 2 < PAIRS:
+                load_x(step + AHEAD + 2)
+            if step < PAIRS:
+                transpose_pair(step)
+                regroup_pair(step)
+            if step == 1:
+                spread_bias()
+            if 1 <= step <= PAIRS:
+                quantise_pair(step - 1)
+                multiply_pair(step - 1)
+            if step >= 2:
+                add_product_pair(step - 2)
+                if step - 2 < PAIRS - 1:
+                    relu_add_vis_pair(step - 2)
+                else:
+                    relu_add_vis_last_pair(step - 2)
+            if 1 <= step <= PAIRS:
+                add_bias_pair(step - 1)
+
+        for n in range(PAIRS):
+            nc.sync.dma_start(out=out[:, objects(n), :], in_=acc_of[n][:])

@@ -26,6 +26,8 @@ QUADRANTS = 4
 PAIR = 2
 PAIRS = OBJECTS // PAIR
 AHEAD = 8
+X_LEAD = 3
+RES_PAIRS = 2
 
 FLOPS = 2 * P * OBJECTS * HEADS * D * DH
 
@@ -36,9 +38,9 @@ def tile_implicitrelationencoder_pb_t_e_kernel(
     nc = tc.nc
     with ExitStack() as ctx:
         const = ctx.enter_context(tc.tile_pool(name="const", bufs=1))
-        x_pool = ctx.enter_context(tc.tile_pool(name="x", bufs=AHEAD + 3))
-        self_pool = ctx.enter_context(tc.tile_pool(name="self", bufs=AHEAD + 2))
-        vis_pool = ctx.enter_context(tc.tile_pool(name="vis", bufs=AHEAD + 3))
+        x_pool = ctx.enter_context(tc.tile_pool(name="x", bufs=AHEAD + X_LEAD + 1))
+        self_pool = ctx.enter_context(tc.tile_pool(name="self", bufs=AHEAD // RES_PAIRS + 2))
+        vis_pool = ctx.enter_context(tc.tile_pool(name="vis", bufs=AHEAD // RES_PAIRS + 2))
         acc_pool = ctx.enter_context(tc.tile_pool(name="acc", bufs=PAIRS))
         mx_pool = ctx.enter_context(tc.tile_pool(name="mx", bufs=3))
         bias_psum = ctx.enter_context(tc.psum_pool(name="bias_psum", bufs=1))
@@ -86,12 +88,14 @@ def tile_implicitrelationencoder_pb_t_e_kernel(
             x_of[n] = x_sb
 
         def load_residuals(n):
-            self_sb = self_pool.tile([P, PAIR, WIDTH], BF16)
-            nc.sync.dma_start(out=self_sb[:], in_=self_feat[:, objects(n), :])
-            self_of[n] = self_sb
-            vis_sb = vis_pool.tile([P, PAIR, WIDTH], BF16)
-            nc.sync.dma_start(out=vis_sb[:], in_=vis[:, objects(n), :])
-            vis_of[n] = vis_sb
+            objs = slice(n * PAIR, (n + RES_PAIRS) * PAIR)
+            self_sb = self_pool.tile([P, RES_PAIRS, PAIR, WIDTH], BF16)
+            nc.sync.dma_start(out=self_sb[:].rearrange("b r j c -> b (r j) c"), in_=self_feat[:, objs, :])
+            vis_sb = vis_pool.tile([P, RES_PAIRS, PAIR, WIDTH], BF16)
+            nc.sync.dma_start(out=vis_sb[:].rearrange("b r j c -> b (r j) c"), in_=vis[:, objs, :])
+            for r in range(RES_PAIRS):
+                self_of[n + r] = self_sb[:, r]
+                vis_of[n + r] = vis_sb[:, r]
 
         def transpose_pair(n):
             x_words = x_of[n][:].bitcast(F32)
@@ -144,7 +148,7 @@ def tile_implicitrelationencoder_pb_t_e_kernel(
             acc = acc_pool.tile([P, PAIR, WIDTH], F32)
             nc.vector.tensor_tensor(
                 out=acc[:],
-                in0=self_of[n][:],
+                in0=self_of[n],
                 in1=bias_all[:].unsqueeze(1).to_broadcast([P, PAIR, WIDTH]),
                 op=ADD,
             )
@@ -161,26 +165,28 @@ def tile_implicitrelationencoder_pb_t_e_kernel(
 
         def relu_add_vis_pair(n):
             nc.scalar.activation(out=acc_of[n][:], in_=acc_of[n][:], func=RELU)
-            nc.gpsimd.tensor_tensor(out=acc_of[n][:], in0=acc_of[n][:], in1=vis_of[n][:], op=ADD)
+            nc.gpsimd.tensor_tensor(out=acc_of[n][:], in0=acc_of[n][:], in1=vis_of[n], op=ADD)
 
         def relu_add_vis_last_pair(n):
             nc.vector.scalar_tensor_tensor(
-                out=acc_of[n][:], in0=acc_of[n][:], scalar=0.0, in1=vis_of[n][:], op0=MAX, op1=ADD
+                out=acc_of[n][:], in0=acc_of[n][:], scalar=0.0, in1=vis_of[n], op0=MAX, op1=ADD
             )
 
         load_x(0)
         load_weight()
         load_x(1)
         nc.sync.dma_start(out=bias_row[0:1, :], in_=out_b.unsqueeze(0))
+        load_x(2)
         for n in range(AHEAD):
-            load_residuals(n)
-            load_x(n + 2)
+            if n % RES_PAIRS == 0:
+                load_residuals(n)
+            load_x(n + X_LEAD)
 
         for step in range(PAIRS + 2):
-            if step + AHEAD < PAIRS:
+            if step + AHEAD < PAIRS and (step + AHEAD) % RES_PAIRS == 0:
                 load_residuals(step + AHEAD)
-            if step + AHEAD + 2 < PAIRS:
-                load_x(step + AHEAD + 2)
+            if step + AHEAD + X_LEAD < PAIRS:
+                load_x(step + AHEAD + X_LEAD)
             if step < PAIRS:
                 transpose_pair(step)
                 regroup_pair(step)

@@ -25,9 +25,9 @@ D_WORDS = D // 2
 QUADRANTS = 4
 PAIR = 2
 PAIRS = OBJECTS // PAIR
-AHEAD = 8
-X_LEAD = 3
-RES_PAIRS = 2
+X_TILE_PAIRS = 4
+X_TILES = 3
+STORES = ((0, 4), (4, 4), (8, 4), (12, 2), (14, 2), (16, 1), (17, 1))
 
 FLOPS = 2 * P * OBJECTS * HEADS * D * DH
 
@@ -38,10 +38,8 @@ def tile_implicitrelationencoder_pb_t_e_kernel(
     nc = tc.nc
     with ExitStack() as ctx:
         const = ctx.enter_context(tc.tile_pool(name="const", bufs=1))
-        x_pool = ctx.enter_context(tc.tile_pool(name="x", bufs=AHEAD + X_LEAD + 1))
-        self_pool = ctx.enter_context(tc.tile_pool(name="self", bufs=AHEAD // RES_PAIRS + 2))
-        vis_pool = ctx.enter_context(tc.tile_pool(name="vis", bufs=AHEAD // RES_PAIRS + 2))
-        acc_pool = ctx.enter_context(tc.tile_pool(name="acc", bufs=PAIRS))
+        x_pool = ctx.enter_context(tc.tile_pool(name="x", bufs=X_TILES))
+        keep = ctx.enter_context(tc.tile_pool(name="keep", bufs=1))
         mx_pool = ctx.enter_context(tc.tile_pool(name="mx", bufs=3))
         bias_psum = ctx.enter_context(tc.psum_pool(name="bias_psum", bufs=1))
         xt_psum = ctx.enter_context(tc.psum_pool(name="xt_psum", bufs=3))
@@ -49,6 +47,10 @@ def tile_implicitrelationencoder_pb_t_e_kernel(
         ctx.enter_context(tc.manual_schedule())
 
         x_of, self_of, vis_of, acc_of = {}, {}, {}, {}
+        x_tile_of = {}
+        acc_all = keep.tile([P, PAIRS, PAIR, WIDTH], F32)
+        for n in range(PAIRS):
+            acc_of[n] = acc_all[:, n]
         xt_of, grouped_of, codes_of, scales_of, prod_of = {}, {}, {}, {}, {}
 
         w_codes = const.tile([P, HEADS, DH], U32, align_bytes=64)
@@ -82,23 +84,36 @@ def tile_implicitrelationencoder_pb_t_e_kernel(
         def objects(n):
             return slice(n * PAIR, (n + 1) * PAIR)
 
-        def load_x(n):
-            x_sb = x_pool.tile([P, PAIR, HEADS * D], BF16)
-            nc.sync.dma_start(out=x_sb[:], in_=out_t[:, objects(n)].rearrange("b n h k -> b n (h k)"))
-            x_of[n] = x_sb
+        def load_x(first, count):
+            t = first // X_TILE_PAIRS
+            if t not in x_tile_of:
+                x_sb = x_pool.tile([P, X_TILE_PAIRS, PAIR, HEADS * D], BF16)
+                x_tile_of[t] = x_sb
+            r = first % X_TILE_PAIRS
+            nc.sync.dma_start(
+                out=x_tile_of[t][:, r : r + count].rearrange("b r j k -> b (r j) k"),
+                in_=out_t[:, first * PAIR : (first + count) * PAIR].rearrange("b n h k -> b n (h k)"),
+            )
+            for i in range(count):
+                x_of[first + i] = x_tile_of[t][:, r + i]
 
-        def load_residuals(n):
-            objs = slice(n * PAIR, (n + RES_PAIRS) * PAIR)
-            self_sb = self_pool.tile([P, RES_PAIRS, PAIR, WIDTH], BF16)
-            nc.sync.dma_start(out=self_sb[:].rearrange("b r j c -> b (r j) c"), in_=self_feat[:, objs, :])
-            vis_sb = vis_pool.tile([P, RES_PAIRS, PAIR, WIDTH], BF16)
-            nc.sync.dma_start(out=vis_sb[:].rearrange("b r j c -> b (r j) c"), in_=vis[:, objs, :])
-            for r in range(RES_PAIRS):
-                self_of[n + r] = self_sb[:, r]
-                vis_of[n + r] = vis_sb[:, r]
+        def load_residual(source, kept_of, label, first, count):
+            res_sb = keep.tile([P, count, PAIR, WIDTH], BF16, name="%s%d" % (label, first))
+            nc.sync.dma_start(
+                out=res_sb[:].rearrange("b r j c -> b (r j) c"),
+                in_=source[:, first * PAIR : (first + count) * PAIR, :],
+            )
+            for i in range(count):
+                kept_of[first + i] = res_sb[:, i]
+
+        def load_self(first, count):
+            load_residual(self_feat, self_of, "self", first, count)
+
+        def load_vis(first, count):
+            load_residual(vis, vis_of, "vis", first, count)
 
         def transpose_pair(n):
-            x_words = x_of[n][:].bitcast(F32)
+            x_words = x_of[n].bitcast(F32)
             for j in range(PAIR):
                 xt = xt_psum.tile([P, HEADS, HALVES, P], F32)
                 for h in range(HEADS):
@@ -145,14 +160,12 @@ def tile_implicitrelationencoder_pb_t_e_kernel(
                 prod_of[n, j] = prod
 
         def add_bias_pair(n):
-            acc = acc_pool.tile([P, PAIR, WIDTH], F32)
             nc.vector.tensor_tensor(
-                out=acc[:],
+                out=acc_of[n],
                 in0=self_of[n],
                 in1=bias_all[:].unsqueeze(1).to_broadcast([P, PAIR, WIDTH]),
                 op=ADD,
             )
-            acc_of[n] = acc
 
         def add_product_pair(n):
             for j in range(PAIR):
@@ -164,29 +177,37 @@ def tile_implicitrelationencoder_pb_t_e_kernel(
                 )
 
         def relu_add_vis_pair(n):
-            nc.scalar.activation(out=acc_of[n][:], in_=acc_of[n][:], func=RELU)
-            nc.gpsimd.tensor_tensor(out=acc_of[n][:], in0=acc_of[n][:], in1=vis_of[n], op=ADD)
+            nc.scalar.activation(out=acc_of[n], in_=acc_of[n], func=RELU)
+            nc.gpsimd.tensor_tensor(out=acc_of[n], in0=acc_of[n], in1=vis_of[n], op=ADD)
 
         def relu_add_vis_last_pair(n):
             nc.vector.scalar_tensor_tensor(
-                out=acc_of[n][:], in0=acc_of[n][:], scalar=0.0, in1=vis_of[n], op0=MAX, op1=ADD
+                out=acc_of[n], in0=acc_of[n], scalar=0.0, in1=vis_of[n], op0=MAX, op1=ADD
             )
 
-        load_x(0)
+        load_x(0, 1)
         load_weight()
-        load_x(1)
+        load_x(1, 1)
         nc.sync.dma_start(out=bias_row[0:1, :], in_=out_b.unsqueeze(0))
-        load_x(2)
-        for n in range(AHEAD):
-            if n % RES_PAIRS == 0:
-                load_residuals(n)
-            load_x(n + X_LEAD)
+        load_self(0, 2)
+        load_x(2, 2)
+        load_vis(0, 2)
+        load_self(2, 4)
+        load_x(4, 2)
+        load_vis(2, 4)
+        load_x(6, 2)
+        load_x(8, 2)
+        load_self(6, 4)
+        load_vis(6, 4)
+        load_x(10, 2)
+        load_self(10, 8)
 
         for step in range(PAIRS + 2):
-            if step + AHEAD < PAIRS and (step + AHEAD) % RES_PAIRS == 0:
-                load_residuals(step + AHEAD)
-            if step + AHEAD + X_LEAD < PAIRS:
-                load_x(step + AHEAD + X_LEAD)
+            if step == X_TILE_PAIRS:
+                load_x(12, 4)
+                load_vis(10, 8)
+            if step == 2 * X_TILE_PAIRS:
+                load_x(16, 2)
             if step < PAIRS:
                 transpose_pair(step)
                 regroup_pair(step)
@@ -204,5 +225,8 @@ def tile_implicitrelationencoder_pb_t_e_kernel(
             if 1 <= step <= PAIRS:
                 add_bias_pair(step - 1)
 
-        for n in range(PAIRS):
-            nc.sync.dma_start(out=out[:, objects(n), :], in_=acc_of[n][:])
+        for first, count in STORES:
+            nc.sync.dma_start(
+                out=out[:, first * PAIR : (first + count) * PAIR, :],
+                in_=acc_all[:, first : first + count].rearrange("b r j c -> b (r j) c"),
+            )

@@ -27,7 +27,8 @@ PAIR = 2
 PAIRS = OBJECTS // PAIR
 X_TILE_PAIRS = 4
 X_TILES = 3
-STORES = ((0, 4), (4, 4), (8, 4), (12, 2), (14, 2), (16, 1), (17, 1))
+STORES = ((0, 8), (8, 8), (16, 8), (24, 4), (28, 2), (30, 1), (31, 1), (32, 1), (33, 1))
+FINE_PAIRS = 2
 
 FLOPS = 2 * P * OBJECTS * HEADS * D * DH
 
@@ -48,6 +49,7 @@ def tile_implicitrelationencoder_pb_t_e_kernel(
 
         x_of, self_of, vis_of, acc_of = {}, {}, {}, {}
         x_tile_of = {}
+        vis_psum_of = {}
         acc_all = keep.tile([P, PAIRS, PAIR, WIDTH], F32)
         for n in range(PAIRS):
             acc_of[n] = acc_all[:, n]
@@ -58,12 +60,14 @@ def tile_implicitrelationencoder_pb_t_e_kernel(
         bias_row = const.tile([P, WIDTH], BF16)
         ones = const.tile([P, P], BF16)
         ident = const.tile([P, P], F32)
+        ident_bf = const.tile([P, P], BF16)
         bias_all = bias_psum.tile([P, WIDTH], F32)
 
         nc.vector.memset(w_scales[:].bitcast(I32), 0)
         nc.vector.memset(bias_row[:], 0.0)
         nc.vector.memset(ones[:], 1.0)
         make_identity(nc, ident[:])
+        make_identity(nc, ident_bf[:])
 
         def load_weight():
             nc.sync.dma_start(
@@ -180,10 +184,29 @@ def tile_implicitrelationencoder_pb_t_e_kernel(
             nc.scalar.activation(out=acc_of[n], in_=acc_of[n], func=RELU)
             nc.gpsimd.tensor_tensor(out=acc_of[n], in0=acc_of[n], in1=vis_of[n], op=ADD)
 
+        def relu_add_vis_pair_by_object(n):
+            for j in range(PAIR):
+                nc.scalar.activation(out=acc_of[n][:, j, :], in_=acc_of[n][:, j, :], func=RELU)
+                nc.gpsimd.tensor_tensor(
+                    out=acc_of[n][:, j, :], in0=acc_of[n][:, j, :], in1=vis_of[n][:, j, :], op=ADD
+                )
+
+        def vis_into_psum(n):
+            for j in range(PAIR):
+                xt = xt_psum.tile([P, WIDTH], F32)
+                nc.tensor.matmul(out=xt[:], lhsT=ident_bf[:], rhs=vis_of[n][:, j, :], start=True, stop=True)
+                vis_psum_of[j] = xt
+
         def relu_add_vis_last_pair(n):
-            nc.vector.scalar_tensor_tensor(
-                out=acc_of[n], in0=acc_of[n], scalar=0.0, in1=vis_of[n], op0=MAX, op1=ADD
-            )
+            for j in range(PAIR):
+                nc.vector.scalar_tensor_tensor(
+                    out=acc_of[n][:, j, :],
+                    in0=acc_of[n][:, j, :],
+                    scalar=0.0,
+                    in1=vis_psum_of[j][:],
+                    op0=MAX,
+                    op1=ADD,
+                )
 
         load_x(0, 1)
         load_weight()
@@ -216,17 +239,21 @@ def tile_implicitrelationencoder_pb_t_e_kernel(
             if 1 <= step <= PAIRS:
                 quantise_pair(step - 1)
                 multiply_pair(step - 1)
+            if step == PAIRS - 1:
+                vis_into_psum(PAIRS - 1)
             if step >= 2:
                 add_product_pair(step - 2)
-                if step - 2 < PAIRS - 1:
+                if step - 2 < PAIRS - 1 - FINE_PAIRS:
                     relu_add_vis_pair(step - 2)
+                elif step - 2 < PAIRS - 1:
+                    relu_add_vis_pair_by_object(step - 2)
                 else:
                     relu_add_vis_last_pair(step - 2)
             if 1 <= step <= PAIRS:
                 add_bias_pair(step - 1)
 
+        results = acc_all[:].rearrange("b r j c -> b (r j) c")
         for first, count in STORES:
-            nc.sync.dma_start(
-                out=out[:, first * PAIR : (first + count) * PAIR, :],
-                in_=acc_all[:, first : first + count].rearrange("b r j c -> b (r j) c"),
-            )
+            nc.sync.dma_start(out=out[:, first : first + count, :], in_=results[:, first : first + count, :])
+        for o in range(OBJECTS - PAIR, OBJECTS):
+            nc.scalar.dma_start(out=out[:, o : o + 1, :], in_=results[:, o : o + 1, :])

@@ -27,7 +27,8 @@ PAIR = 2
 PAIRS = OBJECTS // PAIR
 X_TILE_PAIRS = 4
 X_TILES = 3
-STORES = ((0, 8), (8, 8), (16, 8), (24, 4), (28, 2), (30, 1), (31, 1), (32, 1), (33, 1))
+STORES = ((0, 8), (16, 8), (28, 2), (30, 1), (31, 1), (32, 1), (33, 1))
+SCALAR_STORES = {13: (8, 8), 17: (24, 4)}
 FINE_PAIRS = 2
 
 FLOPS = 2 * P * OBJECTS * HEADS * D * DH
@@ -53,6 +54,7 @@ def tile_implicitrelationencoder_pb_t_e_kernel(
         acc_all = keep.tile([P, PAIRS, PAIR, WIDTH], F32)
         for n in range(PAIRS):
             acc_of[n] = acc_all[:, n]
+        results = acc_all[:].rearrange("b r j c -> b (r j) c")
         xt_of, grouped_of, codes_of, scales_of, prod_of = {}, {}, {}, {}, {}
 
         w_codes = const.tile([P, HEADS, DH], U32, align_bytes=64)
@@ -234,6 +236,9 @@ def tile_implicitrelationencoder_pb_t_e_kernel(
             if step < PAIRS:
                 transpose_pair(step)
                 regroup_pair(step)
+            if step in SCALAR_STORES:
+                first, count = SCALAR_STORES[step]
+                nc.scalar.dma_start(out=out[:, first : first + count, :], in_=results[:, first : first + count, :])
             if step == 1:
                 spread_bias()
             if 1 <= step <= PAIRS:
@@ -252,7 +257,6 @@ def tile_implicitrelationencoder_pb_t_e_kernel(
             if 1 <= step <= PAIRS:
                 add_bias_pair(step - 1)
 
-        results = acc_all[:].rearrange("b r j c -> b (r j) c")
         for first, count in STORES:
             nc.sync.dma_start(out=out[:, first : first + count, :], in_=results[:, first : first + count, :])
         for o in range(OBJECTS - PAIR, OBJECTS):

from contextlib import ExitStack

import concourse.mybir as mybir
from concourse.masks import make_identity

BF16 = mybir.dt.bfloat16
F32 = mybir.dt.float32
I32 = mybir.dt.int32
U32 = mybir.dt.uint32
U8 = mybir.dt.uint8
FP8X4 = mybir.dt.float8_e4m3fn_x4
ADD = mybir.AluOpType.add
MAX = mybir.AluOpType.max
RELU = mybir.ActivationFunctionType.Relu

P = 128
OBJECTS = 36
HEADS = 2
D = 512
DH = 256
WIDTH = HEADS * DH
CODES = 4
HALVES = 2
D_WORDS = D // 2
QUADRANTS = 4
PAIR = 2
PAIRS = OBJECTS // PAIR
X_TILE_PAIRS = 4
X_TILES = 3
STORES = ((0, 8), (16, 8), (28, 2), (30, 1), (31, 1), (32, 1), (33, 1))
SCALAR_STORES = {13: (8, 8), 17: (24, 4)}
FINE_PAIRS = 2

FLOPS = 2 * P * OBJECTS * HEADS * D * DH


def tile_implicitrelationencoder_pb_t_e_kernel(
    tc, out_t, out_w_words, out_w_scales, out_b, self_feat, vis, out
):
    nc = tc.nc
    with ExitStack() as ctx:
        const = ctx.enter_context(tc.tile_pool(name="const", bufs=1))
        x_pool = ctx.enter_context(tc.tile_pool(name="x", bufs=X_TILES))
        keep = ctx.enter_context(tc.tile_pool(name="keep", bufs=1))
        mx_pool = ctx.enter_context(tc.tile_pool(name="mx", bufs=3))
        bias_psum = ctx.enter_context(tc.psum_pool(name="bias_psum", bufs=1))
        xt_psum = ctx.enter_context(tc.psum_pool(name="xt_psum", bufs=3))
        prod_psum = ctx.enter_context(tc.psum_pool(name="prod_psum", bufs=4))
        ctx.enter_context(tc.manual_schedule())

        x_of, self_of, vis_of, acc_of = {}, {}, {}, {}
        x_tile_of = {}
        vis_psum_of = {}
        acc_all = keep.tile([P, PAIRS, PAIR, WIDTH], F32)
        for n in range(PAIRS):
            acc_of[n] = acc_all[:, n]
        results = acc_all[:].rearrange("b r j c -> b (r j) c")
        xt_of, grouped_of, codes_of, scales_of, prod_of = {}, {}, {}, {}, {}

        w_codes = const.tile([P, HEADS, DH], U32, align_bytes=64)
        w_scales = const.tile([P, HEADS, DH], U8, align_bytes=64)
        bias_row = const.tile([P, WIDTH], BF16)
        ones = const.tile([P, P], BF16)
        ident = const.tile([P, P], F32)
        ident_bf = const.tile([P, P], BF16)
        bias_all = bias_psum.tile([P, WIDTH], F32)

        nc.vector.memset(w_scales[:].bitcast(I32), 0)
        nc.vector.memset(bias_row[:], 0.0)
        nc.vector.memset(ones[:], 1.0)
        make_identity(nc, ident[:])
        make_identity(nc, ident_bf[:])

        def load_weight():
            nc.sync.dma_start(
                out=w_codes[:].bitcast(I32),
                in_=out_w_words.rearrange("h p c t -> p h (c t)").bitcast(I32),
            )
            for quadrant in range(QUADRANTS):
                nc.sync.dma_start(
                    out=w_scales[32 * quadrant : 32 * quadrant + 4].bitcast(I32),
                    in_=out_w_scales[:, 4 * quadrant : 4 * quadrant + 4, :]
                    .rearrange("h q c -> q h c")
                    .bitcast(I32),
                )

        def spread_bias():
            nc.tensor.matmul(out=bias_all[:], lhsT=ones[:], rhs=bias_row[:], start=True, stop=True)

        def objects(n):
            return slice(n * PAIR, (n + 1) * PAIR)

        def load_x(first, count):
            t = first // X_TILE_PAIRS
            if t not in x_tile_of:
                x_sb = x_pool.tile([P, X_TILE_PAIRS, PAIR, HEADS * D], BF16)
                x_tile_of[t] = x_sb
            r = first % X_TILE_PAIRS
            nc.sync.dma_start(
                out=x_tile_of[t][:, r : r + count].rearrange("b r j k -> b (r j) k"),
                in_=out_t[:, first * PAIR : (first + count) * PAIR].rearrange("b n h k -> b n (h k)"),
            )
            for i in range(count):
                x_of[first + i] = x_tile_of[t][:, r + i]

        def load_residual(source, kept_of, label, first, count):
            res_sb = keep.tile([P, count, PAIR, WIDTH], BF16, name="%s%d" % (label, first))
            nc.sync.dma_start(
                out=res_sb[:].rearrange("b r j c -> b (r j) c"),
                in_=source[:, first * PAIR : (first + count) * PAIR, :],
            )
            for i in range(count):
                kept_of[first + i] = res_sb[:, i]

        def load_self(first, count):
            load_residual(self_feat, self_of, "self", first, count)

        def load_vis(first, count):
            load_residual(vis, vis_of, "vis", first, count)

        def transpose_pair(n):
            x_words = x_of[n].bitcast(F32)
            for j in range(PAIR):
                xt = xt_psum.tile([P, HEADS, HALVES, P], F32)
                for h in range(HEADS):
                    for u in range(HALVES):
                        nc.tensor.transpose(
                            xt[:, h, u, :],
                            x_words[:, j, h * D_WORDS + u : (h + 1) * D_WORDS : HALVES],
                            ident[:],
                        )
                xt_of[n, j] = xt

        def regroup_pair(n):
            grouped = mx_pool.tile([P, PAIR, HEADS, P, CODES], BF16, align_bytes=64)
            for j in range(PAIR):
                nc.scalar.copy(
                    out=grouped[:].bitcast(F32)[:, j],
                    in_=xt_of[n, j][:].rearrange("p h u b -> p h b u"),
                )
            grouped_of[n] = grouped

        def quantise_pair(n):
            codes = mx_pool.tile([P, PAIR, HEADS, P], U32, align_bytes=64)
            scales = mx_pool.tile([P, PAIR, HEADS, P], U8, align_bytes=64)
            nc.vector.quantize_mx(
                out=codes[:].rearrange("p j h b -> p (j h b)").bitcast(FP8X4),
                scales=scales[:].rearrange("p j h b -> p (j h b)"),
                in_=grouped_of[n][:].rearrange("p j h b t -> p (j h b t)"),
            )
            codes_of[n], scales_of[n] = codes, scales

        def multiply_pair(n):
            for j in range(PAIR):
                prod = prod_psum.tile([P, HEADS, DH], F32)
                for h in range(HEADS):
                    nc.tensor.matmul_mx(
                        out=prod[:, h, :],
                        lhsT=codes_of[n][:, j, h, :].bitcast(FP8X4),
                        lhsT_scale=scales_of[n][:, j, h, :],
                        rhs=w_codes[:, h, :].bitcast(FP8X4),
                        rhs_scale=w_scales[:, h, :],
                        start=True,
                        stop=True,
                    )
                prod_of[n, j] = prod

        def add_bias_pair(n):
            nc.vector.tensor_tensor(
                out=acc_of[n],
                in0=self_of[n],
                in1=bias_all[:].unsqueeze(1).to_broadcast([P, PAIR, WIDTH]),
                op=ADD,
            )

        def add_product_pair(n):
            for j in range(PAIR):
                nc.vector.tensor_tensor(
                    out=acc_of[n][:, j, :],
                    in0=prod_of[n, j][:].rearrange("b h c -> b (h c)"),
                    in1=acc_of[n][:, j, :],
                    op=ADD,
                )

        def relu_add_vis_pair(n):
            nc.scalar.activation(out=acc_of[n], in_=acc_of[n], func=RELU)
            nc.gpsimd.tensor_tensor(out=acc_of[n], in0=acc_of[n], in1=vis_of[n], op=ADD)

        def relu_add_vis_pair_by_object(n):
            for j in range(PAIR):
                nc.scalar.activation(out=acc_of[n][:, j, :], in_=acc_of[n][:, j, :], func=RELU)
                nc.gpsimd.tensor_tensor(
                    out=acc_of[n][:, j, :], in0=acc_of[n][:, j, :], in1=vis_of[n][:, j, :], op=ADD
                )

        def vis_into_psum(n):
            for j in range(PAIR):
                xt = xt_psum.tile([P, WIDTH], F32)
                nc.tensor.matmul(out=xt[:], lhsT=ident_bf[:], rhs=vis_of[n][:, j, :], start=True, stop=True)
                vis_psum_of[j] = xt

        def relu_add_vis_last_pair(n):
            for j in range(PAIR):
                nc.vector.scalar_tensor_tensor(
                    out=acc_of[n][:, j, :],
                    in0=acc_of[n][:, j, :],
                    scalar=0.0,
                    in1=vis_psum_of[j][:],
                    op0=MAX,
                    op1=ADD,
                )

        load_x(0, 1)
        load_weight()
        load_x(1, 1)
        nc.sync.dma_start(out=bias_row[0:1, :], in_=out_b.unsqueeze(0))
        load_self(0, 2)
        load_x(2, 2)
        load_vis(0, 2)
        load_self(2, 4)
        load_x(4, 2)
        load_vis(2, 4)
        load_x(6, 2)
        load_x(8, 2)
        load_self(6, 4)
        load_vis(6, 4)
        load_x(10, 2)
        load_self(10, 8)

        for step in range(PAIRS + 2):
            if step == X_TILE_PAIRS:
                load_x(12, 4)
                load_vis(10, 8)
            if step == 2 * X_TILE_PAIRS:
                load_x(16, 2)
            if step < PAIRS:
                transpose_pair(step)
                regroup_pair(step)
            if step in SCALAR_STORES:
                first, count = SCALAR_STORES[step]
                nc.scalar.dma_start(out=out[:, first : first + count, :], in_=results[:, first : first + count, :])
            if step == 1:
                spread_bias()
            if 1 <= step <= PAIRS:
                quantise_pair(step - 1)
                multiply_pair(step - 1)
            if step == PAIRS - 1:
                vis_into_psum(PAIRS - 1)
            if step >= 2:
                add_product_pair(step - 2)
                if step - 2 < PAIRS - 1 - FINE_PAIRS:
                    relu_add_vis_pair(step - 2)
                elif step - 2 < PAIRS - 1:
                    relu_add_vis_pair_by_object(step - 2)
                else:
                    relu_add_vis_last_pair(step - 2)
            if 1 <= step <= PAIRS:
                add_bias_pair(step - 1)

        for first, count in STORES:
            nc.sync.dma_start(out=out[:, first : first + count, :], in_=results[:, first : first + count, :])
        for o in range(OBJECTS - PAIR, OBJECTS):
            nc.scalar.dma_start(out=out[:, o : o + 1, :], in_=results[:, o : o + 1, :])
